import numpy as np
import ml_dtypes


def mxq(x, axis, fmt="e4m3"):
    dtype, down = {"e4m3": (ml_dtypes.float8_e4m3fn, 7), "e5m2": (ml_dtypes.float8_e5m2, 14)}[fmt]
    v = np.moveaxis(np.asarray(x, np.float32).astype(ml_dtypes.bfloat16).astype(np.float64), axis, -1)
    blocks = v.reshape(v.shape[:-1] + (-1, 32))
    amax = np.abs(blocks).max(-1, keepdims=True)
    byte = np.maximum(np.where(amax > 0, np.frexp(amax)[1] - 1 + 127, 0) - down, 1)
    scale = np.exp2(byte - 127.0)
    codes = (blocks / scale).astype(np.float32).astype(dtype).astype(np.float64)
    return np.moveaxis((codes * scale).reshape(v.shape), -1, axis)


WIDE = False


def mx_kscale(k):
    if not WIDE:
        return np.ones(k)
    levels = np.array([10, -10, 5, -5, 0])
    a = np.random.permutation(np.resize(levels, k // 512 * 4)).reshape(k // 512, 4)
    idx = np.arange(k)
    return np.exp2(a[idx // 512, idx % 128 // 32])


BF16 = ml_dtypes.bfloat16


def bf(x):
    return np.asarray(x, np.float32).astype(BF16)


def f64(x):
    return np.asarray(x).astype(np.float64)


B, N, D, H = 16, 512, 512, 128
EDGE_P = 0.01
DEG = 1.0 + EDGE_P * N


def normalize_adj(adj):
    rowsum = adj.sum(axis=1)
    d_inv_sqrt = np.where(rowsum > 0, 1.0 / np.sqrt(np.maximum(rowsum, 1e-30)), 0.0)
    return d_inv_sqrt[:, :, None] * adj.transpose(0, 2, 1) * d_inv_sqrt[:, None, :]


def setup_inputs():
    s = mx_kscale(D)
    adj = (np.random.uniform(size=(B, N, N)) < EDGE_P).astype(np.float64)
    adj = np.minimum(adj + np.eye(N)[None], 1.0)
    return {"batch_graph": bf(np.random.standard_normal((B, N, D)) * s),
            "adj": bf(adj),
            "W1": bf(np.random.standard_normal((D, H)) * np.sqrt(DEG / D) / s[:, None]),
            "b1": bf(np.random.standard_normal(H) * 0.2)}


def reference(batch_graph, adj, W1, b1):
    a = normalize_adj(f64(adj))
    z = mxq(f64(batch_graph), 2, "e4m3") @ mxq(f64(W1), 0, "e4m3")
    return np.maximum((mxq(a, 2, "e4m3") @ mxq(z, 1, "e4m3")) + f64(b1), 0.0)

@@ -1,0 +1,285 @@
+from contextlib import ExitStack
+
+import concourse.mybir as mybir
+from concourse.masks import make_identity
+
+F32 = mybir.dt.float32
+BF16 = mybir.dt.bfloat16
+U32 = mybir.dt.uint32
+U8 = mybir.dt.uint8
+FP8X4 = mybir.dt.float8_e4m3fn_x4
+ALU = mybir.AluOpType
+ACT = mybir.ActivationFunctionType
+
+P = 128
+PACK = 4
+GRAPHS = 16
+NODES = 512
+FEATS = 512
+HIDDEN = 128
+NODE_TILES = NODES // P
+
+FLOPS = 2 * GRAPHS * NODES * (FEATS + NODES) * HIDDEN
+
+V_COLS = 256
+
+LOAD_AHEAD = 4
+
+
+def tile_perception_pa_t_kernel(tc, batch_graph, adj, W1, b1, out):
+    nc = tc.nc
+    with ExitStack() as ctx:
+        const = ctx.enter_context(tc.tile_pool(name="const", bufs=1))
+        inputs = ctx.enter_context(tc.tile_pool(name="inputs", bufs=GRAPHS))
+        work = ctx.enter_context(tc.tile_pool(name="work", bufs=2))
+        small = ctx.enter_context(tc.tile_pool(name="small", bufs=3))
+        psum = ctx.enter_context(tc.psum_pool(name="psum", bufs=1))
+
+        adj_sb = {}
+        x_sb = {}
+
+        def load_adj(b):
+            adj_rows = inputs.tile([P, PACK, NODES], BF16)
+            nc.sync.dma_start(out=adj_rows[:], in_=adj[b].rearrange("(t p) i -> p t i", p=P))
+            adj_sb[b] = adj_rows
+
+        def load_x(b):
+            x_rows = inputs.tile([P, PACK, FEATS], BF16)
+            nc.sync.dma_start(
+                out=x_rows[:], in_=batch_graph[b].rearrange("(q s) d -> q s d", s=PACK)
+            )
+            x_sb[b] = x_rows
+
+        load_adj(0)
+        w_rows = const.tile([P, PACK, HIDDEN], BF16)
+        for u in range(2):
+            nc.sync.dma_start(
+                out=w_rows[:, 2 * u : 2 * u + 2, :],
+                in_=W1[256 * u : 256 * u + 256, :].rearrange("(q e) h -> q e h", e=2),
+            )
+        bias_rows = const.tile([P, HIDDEN], BF16)
+        nc.vector.memset(bias_rows[:], 0.0)
+        nc.sync.dma_start(out=bias_rows[0:1, :], in_=b1.rearrange("(o h) -> o h", o=1))
+
+        ident = const.tile([P, P], F32)
+        make_identity(nc, ident[:])
+        ones = const.tile([P, 1], BF16)
+        nc.vector.memset(ones[:], 1.0)
+
+        bias_ps = psum.tile([P, NODE_TILES], F32, tag="deg_ps")
+        nc.tensor.matmul(bias_ps[:, 0:1], lhsT=bias_rows[:], rhs=ones[:], start=True, stop=True)
+        bias_col = const.tile([P, 1], F32)
+        nc.vector.tensor_copy(out=bias_col[:], in_=bias_ps[:, 0:1])
+
+        w_grouped = const.tile([P, HIDDEN, PACK], BF16, align_bytes=64)
+        nc.vector.tensor_copy(out=w_grouped[:], in_=w_rows[:].rearrange("q t h -> q h t"))
+        w_codes = const.tile([P, HIDDEN], U32, align_bytes=64)
+        w_scales = const.tile([P, HIDDEN], U8, align_bytes=64)
+        nc.vector.quantize_mx(
+            out=w_codes[:].bitcast(FP8X4),
+            scales=w_scales[:],
+            in_=w_grouped[:].rearrange("q h t -> q (h t)"),
+        )
+
+        x_grouped, x_quant = {}, {}
+        deg_sums, deg_floor, deg_root, deg_col, deg_row = {}, {}, {}, {}, {}
+        z_sums, z_grouped, z_quant = {}, {}, {}
+        a_slots, a_grouped, a_quant = {}, {}, {}
+        out_t_sums, relu_t = {}, {}
+
+        def transpose_x(b):
+            x_words = x_sb[b][:].bitcast(F32)
+            grouped = work.tile([P, NODES, PACK], BF16, align_bytes=64)
+            grouped_words = grouped[:].bitcast(F32).rearrange("w (q s) u -> w q s u", s=PACK)
+            for half in range(2):
+                xt = psum.tile([P, 2, 2, P], F32, tag="xt%d" % half)
+                for s2 in range(2):
+                    for u in range(2):
+                        nc.tensor.transpose(
+                            xt[:, s2, u, :],
+                            x_words[:, 2 * half + s2, P * u : P * u + P],
+                            ident[:],
+                        )
+                nc.scalar.copy(
+                    out=grouped_words[:, :, 2 * half : 2 * half + 2, :],
+                    in_=xt[:].rearrange("w s u q -> w q s u"),
+                )
+            x_grouped[b] = grouped
+
+        def quantise_x(b):
+            x_codes = work.tile([P, NODES], U32, align_bytes=64)
+            x_scales = work.tile([P, NODES], U8, align_bytes=64)
+            nc.vector.quantize_mx(
+                out=x_codes[:].bitcast(FP8X4),
+                scales=x_scales[:],
+                in_=x_grouped[b][:].rearrange("w n t -> w (n t)"),
+            )
+            x_quant[b] = (x_codes, x_scales)
+
+        def first_matmul(b):
+            x_codes, x_scales = x_quant[b]
+            z_ps = psum.tile([P, PACK, HIDDEN], F32)
+            for t in range(PACK):
+                nc.tensor.matmul_mx(
+                    out=z_ps[:, t, :],
+                    lhsT=x_codes[:, P * t : P * t + P].bitcast(FP8X4),
+                    lhsT_scale=x_scales[:, P * t : P * t + P],
+                    rhs=w_codes[:].bitcast(FP8X4),
+                    rhs_scale=w_scales[:],
+                    start=True,
+                    stop=True,
+                )
+            z_sums[b] = z_ps
+
+        def round_z(b):
+            zg = work.tile([P, HIDDEN, PACK], BF16, align_bytes=64)
+            nc.scalar.copy(out=zg[:], in_=z_sums[b][:].rearrange("p t h -> p h t"))
+            z_grouped[b] = zg
+
+        def quantise_z(b):
+            z_codes = work.tile([P, HIDDEN], U32, align_bytes=64, bufs=3)
+            z_scales = work.tile([P, HIDDEN], U8, align_bytes=64, bufs=3)
+            nc.vector.quantize_mx(
+                out=z_codes[:].bitcast(FP8X4),
+                scales=z_scales[:],
+                in_=z_grouped[b][:].rearrange("p h t -> p (h t)"),
+            )
+            z_quant[b] = (z_codes, z_scales)
+
+        def sum_degrees(b):
+            deg_ps = psum.tile([P, NODE_TILES], F32)
+            for f in range(NODE_TILES):
+                for t in range(PACK):
+                    nc.tensor.matmul(
+                        deg_ps[:, f : f + 1],
+                        lhsT=adj_sb[b][:, t, P * f : P * f + P],
+                        rhs=ones[:],
+                        start=(t == 0),
+                        stop=(t == PACK - 1),
+                    )
+            deg_sums[b] = deg_ps
+
+        def floor_degrees(b):
+            floor_c = small.tile([P, NODE_TILES], F32)
+            nc.vector.tensor_scalar_max(out=floor_c[:], in0=deg_sums[b][:], scalar1=1e-30)
+            deg_floor[b] = floor_c
+
+        def root_degrees(b):
+            root_c = small.tile([P, NODE_TILES], F32)
+            nc.scalar.sqrt(out=root_c[:], in_=deg_floor[b][:])
+            deg_root[b] = root_c
+
+        def invert_degrees(b):
+            inv_root = small.tile([P, NODE_TILES], F32)
+            nc.vector.reciprocal(out=inv_root[:], in_=deg_root[b][:])
+            d_col = small.tile([P, NODE_TILES], F32)
+            nc.vector.scalar_tensor_tensor(
+                out=d_col[:], in0=deg_sums[b][:], scalar=0.0, in1=inv_root[:],
+                op0=ALU.is_gt, op1=ALU.mult,
+            )
+            deg_col[b] = d_col
+
+        def spread_degrees(b):
+            d_row = psum.tile([P, NODES], F32, bufs=2)
+            for f in range(NODE_TILES):
+                nc.tensor.transpose(
+                    d_row[:, P * f : P * f + P],
+                    deg_col[b][:, f : f + 1].to_broadcast([P, P]),
+                    ident[:],
+                )
+            deg_row[b] = d_row
+
+        def scale_adj(b):
+            a_rows = work.tile([P, PACK, NODES], BF16)
+            for t in range(PACK):
+                nc.vector.scalar_tensor_tensor(
+                    out=a_rows[:, t, :], in0=adj_sb[b][:, t, :], scalar=deg_col[b][:, t : t + 1],
+                    in1=deg_row[b][:], op0=ALU.mult, op1=ALU.mult,
+                )
+            a_slots[b] = a_rows
+
+        def regroup_a_on_vector(b):
+            ag = work.tile([P, NODES, PACK], BF16, align_bytes=64)
+            nc.vector.tensor_copy(
+                out=ag[:, 0:V_COLS, :].rearrange("p (c i) t -> p c t i", i=4),
+                in_=a_slots[b][:, :, 0:V_COLS].rearrange("p t (c i) -> p c t i", i=4),
+            )
+            a_grouped[b] = ag
+
+        def regroup_a_on_scalar(b):
+            nc.scalar.copy(
+                out=a_grouped[b][:, V_COLS:NODES, :].rearrange("p (c i) t -> p c t i", i=4),
+                in_=a_slots[b][:, :, V_COLS:NODES].rearrange("p t (c i) -> p c t i", i=4),
+            )
+
+        def quantise_a(b):
+            a_codes = work.tile([P, NODES], U32, align_bytes=64)
+            a_scales = work.tile([P, NODES], U8, align_bytes=64)
+            nc.vector.quantize_mx(
+                out=a_codes[:].bitcast(FP8X4),
+                scales=a_scales[:],
+                in_=a_grouped[b][:].rearrange("p i t -> p (i t)"),
+            )
+            a_quant[b] = (a_codes, a_scales)
+
+        def second_matmul(b):
+            z_codes, z_scales = z_quant[b]
+            a_codes, a_scales = a_quant[b]
+            out_t_ps = psum.tile([P, NODES], F32)
+            nc.tensor.matmul_mx(
+                out=out_t_ps[:],
+                lhsT=z_codes[:].bitcast(FP8X4),
+                lhsT_scale=z_scales[:],
+                rhs=a_codes[:].bitcast(FP8X4),
+                rhs_scale=a_scales[:],
+                start=True,
+                stop=True,
+            )
+            out_t_sums[b] = out_t_ps
+
+        def bias_relu(b):
+            rt = work.tile([P, NODE_TILES, P], F32)
+            nc.scalar.activation(
+                out=rt[:], in_=out_t_sums[b][:].rearrange("h (m f) -> h f m", f=NODE_TILES),
+                func=ACT.Relu, bias=bias_col[:, 0:1], scale=1.0,
+            )
+            relu_t[b] = rt
+
+        def transpose_back_and_store(b):
+            out_ps = psum.tile([P, NODE_TILES, HIDDEN], F32)
+            for f in range(NODE_TILES):
+                nc.tensor.transpose(out_ps[:, f, :], relu_t[b][:, f, :], ident[:])
+            result = work.tile([P, NODE_TILES, HIDDEN], F32, bufs=3)
+            nc.scalar.copy(out=result[:], in_=out_ps[:])
+            nc.sync.dma_start(
+                out=out[b].rearrange("(m f) h -> m f h", f=NODE_TILES), in_=result[:]
+            )
+
+        def run(piece, b):
+            if 0 <= b < GRAPHS:
+                piece(b)
+
+        for b in range(LOAD_AHEAD):
+            load_x(b)
+            load_adj(b + 1)
+        with tc.manual_schedule():
+            for b in range(-2, GRAPHS + 3):
+                run(load_x, b + 2 + LOAD_AHEAD)
+                run(load_adj, b + 3 + LOAD_AHEAD)
+                run(first_matmul, b)
+                run(second_matmul, b - 2)
+                run(regroup_a_on_scalar, b - 1)
+                run(scale_adj, b)
+                run(transpose_back_and_store, b - 3)
+                run(transpose_x, b + 1)
+                run(invert_degrees, b + 1)
+                run(quantise_a, b - 1)
+                run(regroup_a_on_vector, b)
+                run(sum_degrees, b + 2)
+                run(floor_degrees, b + 2)
+                run(spread_degrees, b + 1)
+                run(quantise_x, b + 1)
+                run(round_z, b)
+                run(quantise_z, b)
+                run(bias_relu, b - 2)
+                run(root_degrees, b + 2)

@@ -32,7 +32,7 @@ def tile_perception_pa_t_kernel(tc, batch_graph, adj, W1, b1, out):
         const = ctx.enter_context(tc.tile_pool(name="const", bufs=1))
         inputs = ctx.enter_context(tc.tile_pool(name="inputs", bufs=GRAPHS))
         work = ctx.enter_context(tc.tile_pool(name="work", bufs=2))
-        small = ctx.enter_context(tc.tile_pool(name="small", bufs=3))
+        small = ctx.enter_context(tc.tile_pool(name="small", bufs=4))
         psum = ctx.enter_context(tc.psum_pool(name="psum", bufs=1))
 
         adj_sb = {}
@@ -51,6 +51,7 @@ def tile_perception_pa_t_kernel(tc, batch_graph, adj, W1, b1, out):
             x_sb[b] = x_rows
 
         load_adj(0)
+        load_x(0)
         w_rows = const.tile([P, PACK, HIDDEN], BF16)
         for u in range(2):
             nc.sync.dma_start(
@@ -60,6 +61,9 @@ def tile_perception_pa_t_kernel(tc, batch_graph, adj, W1, b1, out):
         bias_rows = const.tile([P, HIDDEN], BF16)
         nc.vector.memset(bias_rows[:], 0.0)
         nc.sync.dma_start(out=bias_rows[0:1, :], in_=b1.rearrange("(o h) -> o h", o=1))
+        for b in range(1, LOAD_AHEAD):
+            load_adj(b)
+            load_x(b)
 
         ident = const.tile([P, P], F32)
         make_identity(nc, ident[:])
@@ -259,27 +263,24 @@ def tile_perception_pa_t_kernel(tc, batch_graph, adj, W1, b1, out):
             if 0 <= b < GRAPHS:
                 piece(b)
 
-        for b in range(LOAD_AHEAD):
-            load_x(b)
-            load_adj(b + 1)
         with tc.manual_schedule():
-            for b in range(-2, GRAPHS + 3):
-                run(load_x, b + 2 + LOAD_AHEAD)
-                run(load_adj, b + 3 + LOAD_AHEAD)
-                run(first_matmul, b)
-                run(second_matmul, b - 2)
-                run(regroup_a_on_scalar, b - 1)
-                run(scale_adj, b)
-                run(transpose_back_and_store, b - 3)
-                run(transpose_x, b + 1)
-                run(invert_degrees, b + 1)
-                run(quantise_a, b - 1)
-                run(regroup_a_on_vector, b)
-                run(sum_degrees, b + 2)
-                run(floor_degrees, b + 2)
-                run(spread_degrees, b + 1)
-                run(quantise_x, b + 1)
-                run(round_z, b)
-                run(quantise_z, b)
-                run(bias_relu, b - 2)
-                run(root_degrees, b + 2)
+            for s in range(-3, GRAPHS + 3):
+                run(load_adj, s + 3 + LOAD_AHEAD)
+                run(load_x, s + 3 + LOAD_AHEAD)
+                run(floor_degrees, s + 2)
+                run(first_matmul, s + 1)
+                run(second_matmul, s - 2)
+                run(regroup_a_on_scalar, s - 1)
+                run(root_degrees, s + 2)
+                run(quantise_x, s + 2)
+                run(round_z, s + 1)
+                run(bias_relu, s - 2)
+                run(scale_adj, s)
+                run(transpose_x, s + 3)
+                run(invert_degrees, s + 2)
+                run(spread_degrees, s + 1)
+                run(quantise_a, s - 1)
+                run(transpose_back_and_store, s - 3)
+                run(regroup_a_on_vector, s)
+                run(sum_degrees, s + 3)
+                run(quantise_z, s)

@@ -51,18 +51,19 @@ def tile_perception_pa_t_kernel(tc, batch_graph, adj, W1, b1, out):
             x_sb[b] = x_rows
 
         load_adj(0)
+        load_adj(1)
         load_x(0)
         w_rows = const.tile([P, PACK, HIDDEN], BF16)
         for u in range(2):
-            nc.sync.dma_start(
+            nc.scalar.dma_start(
                 out=w_rows[:, 2 * u : 2 * u + 2, :],
                 in_=W1[256 * u : 256 * u + 256, :].rearrange("(q e) h -> q e h", e=2),
             )
         bias_rows = const.tile([P, HIDDEN], BF16)
         nc.vector.memset(bias_rows[:], 0.0)
-        nc.sync.dma_start(out=bias_rows[0:1, :], in_=b1.rearrange("(o h) -> o h", o=1))
+        nc.scalar.dma_start(out=bias_rows[0:1, :], in_=b1.rearrange("(o h) -> o h", o=1))
         for b in range(1, LOAD_AHEAD):
-            load_adj(b)
+            load_adj(b + 1)
             load_x(b)
 
         ident = const.tile([P, P], F32)
@@ -70,7 +71,7 @@ def tile_perception_pa_t_kernel(tc, batch_graph, adj, W1, b1, out):
         ones = const.tile([P, 1], BF16)
         nc.vector.memset(ones[:], 1.0)
 
-        bias_ps = psum.tile([P, NODE_TILES], F32, tag="deg_ps")
+        bias_ps = psum.tile([P, NODE_TILES], F32, tag="deg_ps", bufs=2)
         nc.tensor.matmul(bias_ps[:, 0:1], lhsT=bias_rows[:], rhs=ones[:], start=True, stop=True)
         bias_col = const.tile([P, 1], F32)
         nc.vector.tensor_copy(out=bias_col[:], in_=bias_ps[:, 0:1])
@@ -151,7 +152,7 @@ def tile_perception_pa_t_kernel(tc, batch_graph, adj, W1, b1, out):
             z_quant[b] = (z_codes, z_scales)
 
         def sum_degrees(b):
-            deg_ps = psum.tile([P, NODE_TILES], F32)
+            deg_ps = psum.tile([P, NODE_TILES], F32, bufs=2)
             for f in range(NODE_TILES):
                 for t in range(PACK):
                     nc.tensor.matmul(
@@ -184,7 +185,7 @@ def tile_perception_pa_t_kernel(tc, batch_graph, adj, W1, b1, out):
             deg_col[b] = d_col
 
         def spread_degrees(b):
-            d_row = psum.tile([P, NODES], F32, bufs=2)
+            d_row = psum.tile([P, NODES], F32)
             for f in range(NODE_TILES):
                 nc.tensor.transpose(
                     d_row[:, P * f : P * f + P],
@@ -264,23 +265,23 @@ def tile_perception_pa_t_kernel(tc, batch_graph, adj, W1, b1, out):
                 piece(b)
 
         with tc.manual_schedule():
-            for s in range(-3, GRAPHS + 3):
+            for s in range(-2, GRAPHS + 3):
                 run(load_adj, s + 3 + LOAD_AHEAD)
-                run(load_x, s + 3 + LOAD_AHEAD)
-                run(floor_degrees, s + 2)
-                run(first_matmul, s + 1)
+                run(load_x, s + 2 + LOAD_AHEAD)
+                run(floor_degrees, s + 1)
+                run(first_matmul, s - 1)
                 run(second_matmul, s - 2)
-                run(regroup_a_on_scalar, s - 1)
-                run(root_degrees, s + 2)
-                run(quantise_x, s + 2)
-                run(round_z, s + 1)
-                run(bias_relu, s - 2)
+                run(sum_degrees, s + 2)
                 run(scale_adj, s)
-                run(transpose_x, s + 3)
-                run(invert_degrees, s + 2)
-                run(spread_degrees, s + 1)
-                run(quantise_a, s - 1)
+                run(regroup_a_on_scalar, s - 1)
+                run(round_z, s - 1)
+                run(root_degrees, s + 1)
+                run(bias_relu, s - 2)
+                run(invert_degrees, s + 1)
+                run(transpose_x, s + 1)
+                run(quantise_x, s)
                 run(transpose_back_and_store, s - 3)
+                run(spread_degrees, s + 1)
+                run(quantise_z, s - 1)
+                run(quantise_a, s - 1)
                 run(regroup_a_on_vector, s)
-                run(sum_degrees, s + 3)
-                run(quantise_z, s)

@@ -21,7 +21,7 @@ NODE_TILES = NODES // P
 
 FLOPS = 2 * GRAPHS * NODES * (FEATS + NODES) * HIDDEN
 
-V_COLS = 256
+S_COLS = 256
 
 LOAD_AHEAD = 4
 
@@ -50,9 +50,6 @@ def tile_perception_pa_t_kernel(tc, batch_graph, adj, W1, b1, out):
             )
             x_sb[b] = x_rows
 
-        load_adj(0)
-        load_adj(1)
-        load_x(0)
         w_rows = const.tile([P, PACK, HIDDEN], BF16)
         for u in range(2):
             nc.scalar.dma_start(
@@ -62,7 +59,8 @@ def tile_perception_pa_t_kernel(tc, batch_graph, adj, W1, b1, out):
         bias_rows = const.tile([P, HIDDEN], BF16)
         nc.vector.memset(bias_rows[:], 0.0)
         nc.scalar.dma_start(out=bias_rows[0:1, :], in_=b1.rearrange("(o h) -> o h", o=1))
-        for b in range(1, LOAD_AHEAD):
+        load_adj(0)
+        for b in range(LOAD_AHEAD):
             load_adj(b + 1)
             load_x(b)
 
@@ -203,18 +201,19 @@ def tile_perception_pa_t_kernel(tc, batch_graph, adj, W1, b1, out):
                 )
             a_slots[b] = a_rows
 
-        def regroup_a_on_vector(b):
-            ag = work.tile([P, NODES, PACK], BF16, align_bytes=64)
-            nc.vector.tensor_copy(
-                out=ag[:, 0:V_COLS, :].rearrange("p (c i) t -> p c t i", i=4),
-                in_=a_slots[b][:, :, 0:V_COLS].rearrange("p t (c i) -> p c t i", i=4),
+        def regroup_a_on_scalar(b):
+            ag = work.tile([P, NODES, PACK], BF16, align_bytes=64, bufs=1)
+            nc.scalar.copy(
+                out=ag[:, 0:S_COLS, :].rearrange("p (c i) t -> p c t i", i=4),
+                in_=a_slots[b][:, :, 0:S_COLS].rearrange("p t (c i) -> p c t i", i=4),
             )
             a_grouped[b] = ag
 
-        def regroup_a_on_scalar(b):
-            nc.scalar.copy(
-                out=a_grouped[b][:, V_COLS:NODES, :].rearrange("p (c i) t -> p c t i", i=4),
-                in_=a_slots[b][:, :, V_COLS:NODES].rearrange("p t (c i) -> p c t i", i=4),
+        def regroup_a_on_gpsimd(b):
+            nc.gpsimd.tensor_scalar(
+                out=a_grouped[b][:, S_COLS:NODES, :].rearrange("p (c i) t -> p c t i", i=4),
+                in0=a_slots[b][:, :, S_COLS:NODES].rearrange("p t (c i) -> p c t i", i=4),
+                scalar1=1.0, scalar2=0.0, op0=ALU.mult, op1=ALU.add,
             )
 
         def quantise_a(b):
@@ -274,6 +273,7 @@ def tile_perception_pa_t_kernel(tc, batch_graph, adj, W1, b1, out):
                 run(sum_degrees, s + 2)
                 run(scale_adj, s)
                 run(regroup_a_on_scalar, s - 1)
+                run(regroup_a_on_gpsimd, s - 1)
                 run(round_z, s - 1)
                 run(root_degrees, s + 1)
                 run(bias_relu, s - 2)
@@ -284,4 +284,3 @@ def tile_perception_pa_t_kernel(tc, batch_graph, adj, W1, b1, out):
                 run(spread_degrees, s + 1)
                 run(quantise_z, s - 1)
                 run(quantise_a, s - 1)
-                run(regroup_a_on_vector, s)

@@ -23,6 +23,8 @@ FLOPS = 2 * GRAPHS * NODES * (FEATS + NODES) * HIDDEN
 
 S_COLS = 256
 
+DEG_COLS = 24
+
 LOAD_AHEAD = 4
 
 
@@ -66,13 +68,13 @@ def tile_perception_pa_t_kernel(tc, batch_graph, adj, W1, b1, out):
 
         ident = const.tile([P, P], F32)
         make_identity(nc, ident[:])
-        ones = const.tile([P, 1], BF16)
+        ones = const.tile([P, DEG_COLS], BF16)
         nc.vector.memset(ones[:], 1.0)
 
-        bias_ps = psum.tile([P, NODE_TILES], F32, tag="deg_ps", bufs=2)
-        nc.tensor.matmul(bias_ps[:, 0:1], lhsT=bias_rows[:], rhs=ones[:], start=True, stop=True)
+        bias_ps = psum.tile([P, NODE_TILES, DEG_COLS], F32, tag="deg_ps", bufs=2)
+        nc.tensor.matmul(bias_ps[:, 0, :], lhsT=bias_rows[:], rhs=ones[:], start=True, stop=True)
         bias_col = const.tile([P, 1], F32)
-        nc.vector.tensor_copy(out=bias_col[:], in_=bias_ps[:, 0:1])
+        nc.vector.tensor_copy(out=bias_col[:], in_=bias_ps[:, 0, 0:1])
 
         w_grouped = const.tile([P, HIDDEN, PACK], BF16, align_bytes=64)
         nc.vector.tensor_copy(out=w_grouped[:], in_=w_rows[:].rearrange("q t h -> q h t"))
@@ -150,21 +152,21 @@ def tile_perception_pa_t_kernel(tc, batch_graph, adj, W1, b1, out):
             z_quant[b] = (z_codes, z_scales)
 
         def sum_degrees(b):
-            deg_ps = psum.tile([P, NODE_TILES], F32, bufs=2)
+            deg_ps = psum.tile([P, NODE_TILES, DEG_COLS], F32, bufs=2)
             for f in range(NODE_TILES):
                 for t in range(PACK):
                     nc.tensor.matmul(
-                        deg_ps[:, f : f + 1],
+                        deg_ps[:, f, :],
                         lhsT=adj_sb[b][:, t, P * f : P * f + P],
                         rhs=ones[:],
                         start=(t == 0),
                         stop=(t == PACK - 1),
                     )
-            deg_sums[b] = deg_ps
+            deg_sums[b] = deg_ps[:, :, 0]
 
         def floor_degrees(b):
             floor_c = small.tile([P, NODE_TILES], F32)
-            nc.vector.tensor_scalar_max(out=floor_c[:], in0=deg_sums[b][:], scalar1=1e-30)
+            nc.vector.tensor_scalar_max(out=floor_c[:], in0=deg_sums[b], scalar1=1e-30)
             deg_floor[b] = floor_c
 
         def root_degrees(b):
@@ -177,7 +179,7 @@ def tile_perception_pa_t_kernel(tc, batch_graph, adj, W1, b1, out):
             nc.vector.reciprocal(out=inv_root[:], in_=deg_root[b][:])
             d_col = small.tile([P, NODE_TILES], F32)
             nc.vector.scalar_tensor_tensor(
-                out=d_col[:], in0=deg_sums[b][:], scalar=0.0, in1=inv_root[:],
+                out=d_col[:], in0=deg_sums[b], scalar=0.0, in1=inv_root[:],
                 op0=ALU.is_gt, op1=ALU.mult,
             )
             deg_col[b] = d_col

@@ -21,7 +21,7 @@ NODE_TILES = NODES // P
 
 FLOPS = 2 * GRAPHS * NODES * (FEATS + NODES) * HIDDEN
 
-S_COLS = 256
+S_COLS = 192
 
 DEG_COLS = 24
 
@@ -70,6 +70,11 @@ def tile_perception_pa_t_kernel(tc, batch_graph, adj, W1, b1, out):
         make_identity(nc, ident[:])
         ones = const.tile([P, DEG_COLS], BF16)
         nc.vector.memset(ones[:], 1.0)
+
+        one_col = const.tile([P, 1], F32)
+        nc.vector.memset(one_col[:], 1.0)
+        root_of_one = const.tile([P, 1], F32)
+        nc.scalar.sqrt(out=root_of_one[:], in_=one_col[:])
 
         bias_ps = psum.tile([P, NODE_TILES, DEG_COLS], F32, tag="deg_ps", bufs=2)
         nc.tensor.matmul(bias_ps[:, 0, :], lhsT=bias_rows[:], rhs=ones[:], start=True, stop=True)
@@ -272,7 +277,6 @@ def tile_perception_pa_t_kernel(tc, batch_graph, adj, W1, b1, out):
                 run(floor_degrees, s + 1)
                 run(first_matmul, s - 1)
                 run(second_matmul, s - 2)
-                run(sum_degrees, s + 2)
                 run(scale_adj, s)
                 run(regroup_a_on_scalar, s - 1)
                 run(regroup_a_on_gpsimd, s - 1)
@@ -283,6 +287,7 @@ def tile_perception_pa_t_kernel(tc, batch_graph, adj, W1, b1, out):
                 run(transpose_x, s + 1)
                 run(quantise_x, s)
                 run(transpose_back_and_store, s - 3)
+                run(sum_degrees, s + 2)
                 run(spread_degrees, s + 1)
                 run(quantise_z, s - 1)
                 run(quantise_a, s - 1)

@@ -52,19 +52,19 @@ def tile_perception_pa_t_kernel(tc, batch_graph, adj, W1, b1, out):
             )
             x_sb[b] = x_rows
 
+        load_adj(0)
         w_rows = const.tile([P, PACK, HIDDEN], BF16)
         for u in range(2):
-            nc.scalar.dma_start(
+            nc.sync.dma_start(
                 out=w_rows[:, 2 * u : 2 * u + 2, :],
                 in_=W1[256 * u : 256 * u + 256, :].rearrange("(q e) h -> q e h", e=2),
             )
         bias_rows = const.tile([P, HIDDEN], BF16)
         nc.vector.memset(bias_rows[:], 0.0)
         nc.scalar.dma_start(out=bias_rows[0:1, :], in_=b1.rearrange("(o h) -> o h", o=1))
-        load_adj(0)
         for b in range(LOAD_AHEAD):
-            load_adj(b + 1)
             load_x(b)
+            load_adj(b + 1)
 
         ident = const.tile([P, P], F32)
         make_identity(nc, ident[:])
@@ -74,12 +74,16 @@ def tile_perception_pa_t_kernel(tc, batch_graph, adj, W1, b1, out):
         one_col = const.tile([P, 1], F32)
         nc.vector.memset(one_col[:], 1.0)
         root_of_one = const.tile([P, 1], F32)
-        nc.scalar.sqrt(out=root_of_one[:], in_=one_col[:])
+        nc.scalar.activation(
+            out=root_of_one[:], in_=one_col[:], func=ACT.Abs_reciprocal_sqrt, scale=1.0, bias=0.0
+        )
 
-        bias_ps = psum.tile([P, NODE_TILES, DEG_COLS], F32, tag="deg_ps", bufs=2)
-        nc.tensor.matmul(bias_ps[:, 0, :], lhsT=bias_rows[:], rhs=ones[:], start=True, stop=True)
         bias_col = const.tile([P, 1], F32)
-        nc.vector.tensor_copy(out=bias_col[:], in_=bias_ps[:, 0, 0:1])
+
+        def spread_bias():
+            bias_ps = psum.tile([P, DEG_COLS], F32, tag="out_ps")
+            nc.tensor.matmul(bias_ps[:], lhsT=bias_rows[:], rhs=ones[:], start=True, stop=True)
+            nc.vector.tensor_copy(out=bias_col[:], in_=bias_ps[:, 0:1])
 
         w_grouped = const.tile([P, HIDDEN, PACK], BF16, align_bytes=64)
         nc.vector.tensor_copy(out=w_grouped[:], in_=w_rows[:].rearrange("q t h -> q h t"))
@@ -92,7 +96,7 @@ def tile_perception_pa_t_kernel(tc, batch_graph, adj, W1, b1, out):
         )
 
         x_grouped, x_quant = {}, {}
-        deg_sums, deg_floor, deg_root, deg_col, deg_row = {}, {}, {}, {}, {}
+        deg_sums, deg_root, deg_col, deg_row = {}, {}, {}, {}
         z_sums, z_grouped, z_quant = {}, {}, {}
         a_slots, a_grouped, a_quant = {}, {}, {}
         out_t_sums, relu_t = {}, {}
@@ -157,7 +161,7 @@ def tile_perception_pa_t_kernel(tc, batch_graph, adj, W1, b1, out):
             z_quant[b] = (z_codes, z_scales)
 
         def sum_degrees(b):
-            deg_ps = psum.tile([P, NODE_TILES, DEG_COLS], F32, bufs=2)
+            deg_ps = psum.tile([P, NODE_TILES, DEG_COLS], F32)
             for f in range(NODE_TILES):
                 for t in range(PACK):
                     nc.tensor.matmul(
@@ -169,32 +173,27 @@ def tile_perception_pa_t_kernel(tc, batch_graph, adj, W1, b1, out):
                     )
             deg_sums[b] = deg_ps[:, :, 0]
 
-        def floor_degrees(b):
-            floor_c = small.tile([P, NODE_TILES], F32)
-            nc.vector.tensor_scalar_max(out=floor_c[:], in0=deg_sums[b], scalar1=1e-30)
-            deg_floor[b] = floor_c
-
         def root_degrees(b):
-            root_c = small.tile([P, NODE_TILES], F32)
-            nc.scalar.sqrt(out=root_c[:], in_=deg_floor[b][:])
-            deg_root[b] = root_c
-
-        def invert_degrees(b):
             inv_root = small.tile([P, NODE_TILES], F32)
-            nc.vector.reciprocal(out=inv_root[:], in_=deg_root[b][:])
+            nc.scalar.activation(
+                out=inv_root[:], in_=deg_sums[b], func=ACT.Abs_reciprocal_sqrt, scale=1.0, bias=1e-30
+            )
+            deg_root[b] = inv_root
+
+        def mask_degrees(b):
             d_col = small.tile([P, NODE_TILES], F32)
             nc.vector.scalar_tensor_tensor(
-                out=d_col[:], in0=deg_sums[b], scalar=0.0, in1=inv_root[:],
+                out=d_col[:], in0=deg_sums[b], scalar=0.0, in1=deg_root[b][:],
                 op0=ALU.is_gt, op1=ALU.mult,
             )
             deg_col[b] = d_col
 
         def spread_degrees(b):
-            d_row = psum.tile([P, NODES], F32)
+            d_row = psum.tile([P, NODES], F32, bufs=2)
             for f in range(NODE_TILES):
                 nc.tensor.transpose(
                     d_row[:, P * f : P * f + P],
-                    deg_col[b][:, f : f + 1].to_broadcast([P, P]),
+                    deg_root[b][:, f : f + 1].to_broadcast([P, P]),
                     ident[:],
                 )
             deg_row[b] = d_row
@@ -274,20 +273,21 @@ def tile_perception_pa_t_kernel(tc, batch_graph, adj, W1, b1, out):
             for s in range(-2, GRAPHS + 3):
                 run(load_adj, s + 3 + LOAD_AHEAD)
                 run(load_x, s + 2 + LOAD_AHEAD)
-                run(floor_degrees, s + 1)
-                run(first_matmul, s - 1)
                 run(second_matmul, s - 2)
+                run(spread_degrees, s + 1)
                 run(scale_adj, s)
                 run(regroup_a_on_scalar, s - 1)
                 run(regroup_a_on_gpsimd, s - 1)
-                run(round_z, s - 1)
-                run(root_degrees, s + 1)
                 run(bias_relu, s - 2)
-                run(invert_degrees, s + 1)
+                run(round_z, s - 1)
+                run(mask_degrees, s + 1)
                 run(transpose_x, s + 1)
                 run(quantise_x, s)
                 run(transpose_back_and_store, s - 3)
                 run(sum_degrees, s + 2)
-                run(spread_degrees, s + 1)
+                run(root_degrees, s + 2)
                 run(quantise_z, s - 1)
                 run(quantise_a, s - 1)
+                run(first_matmul, s)
+                if s == 0:
+                    spread_bias()

@@ -23,6 +23,8 @@ FLOPS = 2 * GRAPHS * NODES * (FEATS + NODES) * HIDDEN
 
 S_COLS = 192
 
+TAIL_COLS = 160
+
 DEG_COLS = 24
 
 LOAD_AHEAD = 4
@@ -198,44 +200,52 @@ def tile_perception_pa_t_kernel(tc, batch_graph, adj, W1, b1, out):
                 )
             deg_row[b] = d_row
 
-        def scale_adj(b):
-            a_rows = work.tile([P, PACK, NODES], BF16)
+        def scale_adj(b, i0=0, n=NODES):
+            a_rows = work.tile([P, PACK, n], BF16)
             for t in range(PACK):
                 nc.vector.scalar_tensor_tensor(
-                    out=a_rows[:, t, :], in0=adj_sb[b][:, t, :], scalar=deg_col[b][:, t : t + 1],
-                    in1=deg_row[b][:], op0=ALU.mult, op1=ALU.mult,
+                    out=a_rows[:, t, :], in0=adj_sb[b][:, t, i0 : i0 + n],
+                    scalar=deg_col[b][:, t : t + 1], in1=deg_row[b][:, i0 : i0 + n],
+                    op0=ALU.mult, op1=ALU.mult,
                 )
-            a_slots[b] = a_rows
+            a_slots[b, i0] = a_rows
 
-        def regroup_a_on_scalar(b):
-            ag = work.tile([P, NODES, PACK], BF16, align_bytes=64, bufs=1)
-            nc.scalar.copy(
-                out=ag[:, 0:S_COLS, :].rearrange("p (c i) t -> p c t i", i=4),
-                in_=a_slots[b][:, :, 0:S_COLS].rearrange("p t (c i) -> p c t i", i=4),
+        def regroup_a(b, i0, lo, hi, copy_on):
+            copy_on(
+                a_grouped[b, i0][:, lo:hi, :].rearrange("p (c i) t -> p c t i", i=4),
+                a_slots[b, i0][:, :, lo:hi].rearrange("p t (c i) -> p c t i", i=4),
             )
-            a_grouped[b] = ag
 
-        def regroup_a_on_gpsimd(b):
+        def on_scalar(dst, src):
+            nc.scalar.copy(out=dst, in_=src)
+
+        def on_vector(dst, src):
+            nc.vector.tensor_copy(out=dst, in_=src)
+
+        def on_gpsimd(dst, src):
             nc.gpsimd.tensor_scalar(
-                out=a_grouped[b][:, S_COLS:NODES, :].rearrange("p (c i) t -> p c t i", i=4),
-                in0=a_slots[b][:, :, S_COLS:NODES].rearrange("p t (c i) -> p c t i", i=4),
-                scalar1=1.0, scalar2=0.0, op0=ALU.mult, op1=ALU.add,
+                out=dst, in0=src, scalar1=1.0, scalar2=0.0, op0=ALU.mult, op1=ALU.add
             )
 
-        def quantise_a(b):
-            a_codes = work.tile([P, NODES], U32, align_bytes=64)
-            a_scales = work.tile([P, NODES], U8, align_bytes=64)
+        def regroup_whole(b):
+            ag = work.tile([P, NODES, PACK], BF16, align_bytes=64, bufs=1)
+            a_grouped[b, 0] = ag
+            regroup_a(b, 0, 0, S_COLS, on_scalar)
+            regroup_a(b, 0, S_COLS, NODES, on_gpsimd)
+
+        def quantise_a(b, i0=0, n=NODES):
+            a_codes = work.tile([P, n], U32, align_bytes=64)
+            a_scales = work.tile([P, n], U8, align_bytes=64)
             nc.vector.quantize_mx(
                 out=a_codes[:].bitcast(FP8X4),
                 scales=a_scales[:],
-                in_=a_grouped[b][:].rearrange("p i t -> p (i t)"),
+                in_=a_grouped[b, i0][:].rearrange("p i t -> p (i t)"),
             )
-            a_quant[b] = (a_codes, a_scales)
+            a_quant[b, i0] = (a_codes, a_scales)
 
-        def second_matmul(b):
+        def multiply_a_z(b, i0, out_t_ps):
             z_codes, z_scales = z_quant[b]
-            a_codes, a_scales = a_quant[b]
-            out_t_ps = psum.tile([P, NODES], F32)
+            a_codes, a_scales = a_quant[b, i0]
             nc.tensor.matmul_mx(
                 out=out_t_ps[:],
                 lhsT=z_codes[:].bitcast(FP8X4),
@@ -245,49 +255,112 @@ def tile_perception_pa_t_kernel(tc, batch_graph, adj, W1, b1, out):
                 start=True,
                 stop=True,
             )
-            out_t_sums[b] = out_t_ps
+            out_t_sums[b, i0] = out_t_ps
+
+        def second_matmul(b):
+            out_t_ps = psum.tile([P, NODES], F32)
+            multiply_a_z(b, 0, out_t_ps)
 
         def bias_relu(b):
             rt = work.tile([P, NODE_TILES, P], F32)
             nc.scalar.activation(
-                out=rt[:], in_=out_t_sums[b][:].rearrange("h (m f) -> h f m", f=NODE_TILES),
+                out=rt[:], in_=out_t_sums[b, 0][:].rearrange("h (m f) -> h f m", f=NODE_TILES),
                 func=ACT.Relu, bias=bias_col[:, 0:1], scale=1.0,
             )
-            relu_t[b] = rt
+            relu_t[b, 0] = rt
+
+        def transpose_back(b, i0, out_ps, copy_on):
+            r = out_ps.shape[1]
+            for f in range(r):
+                nc.tensor.transpose(out_ps[:, f, :], relu_t[b, i0][:, f, :], ident[:])
+            result = work.tile([P, r, HIDDEN], F32, bufs=3)
+            copy_on(result[:], out_ps[:])
+            nc.sync.dma_start(
+                out=out[b, i0 : i0 + r * P, :].rearrange("(m f) h -> m f h", f=r), in_=result[:]
+            )
 
         def transpose_back_and_store(b):
             out_ps = psum.tile([P, NODE_TILES, HIDDEN], F32)
-            for f in range(NODE_TILES):
-                nc.tensor.transpose(out_ps[:, f, :], relu_t[b][:, f, :], ident[:])
-            result = work.tile([P, NODE_TILES, HIDDEN], F32, bufs=3)
-            nc.scalar.copy(out=result[:], in_=out_ps[:])
-            nc.sync.dma_start(
-                out=out[b].rearrange("(m f) h -> m f h", f=NODE_TILES), in_=result[:]
-            )
+            transpose_back(b, 0, out_ps, on_scalar)
 
         def run(piece, b):
             if 0 <= b < GRAPHS:
                 piece(b)
 
         with tc.manual_schedule():
-            for s in range(-2, GRAPHS + 3):
-                run(load_adj, s + 3 + LOAD_AHEAD)
-                run(load_x, s + 2 + LOAD_AHEAD)
+            sum_degrees(0)
+            root_degrees(0)
+            spread_degrees(0)
+            mask_degrees(0)
+            transpose_x(0)
+            sum_degrees(1)
+            root_degrees(1)
+            transpose_x(1)
+
+            last = GRAPHS - 1
+            for s in range(last):
+                run(load_adj, s + 1 + LOAD_AHEAD)
+                run(load_x, s + LOAD_AHEAD)
                 run(second_matmul, s - 2)
                 run(spread_degrees, s + 1)
                 run(scale_adj, s)
-                run(regroup_a_on_scalar, s - 1)
-                run(regroup_a_on_gpsimd, s - 1)
+                run(regroup_whole, s - 1)
                 run(bias_relu, s - 2)
-                run(round_z, s - 1)
+                if s == 0:
+                    quantise_x(0)
+                if s == 1:
+                    round_z(0)
+                    first_matmul(1)
+                if s > 0:
+                    round_z(s)
                 run(mask_degrees, s + 1)
-                run(transpose_x, s + 1)
-                run(quantise_x, s)
+                run(transpose_x, s + 2)
+                run(quantise_x, s + 1)
                 run(transpose_back_and_store, s - 3)
                 run(sum_degrees, s + 2)
                 run(root_degrees, s + 2)
-                run(quantise_z, s - 1)
+                if s == 1:
+                    quantise_z(0)
+                if s > 0:
+                    quantise_z(s)
                 run(quantise_a, s - 1)
-                run(first_matmul, s)
+                first_matmul(0 if s == 0 else s + 1)
                 if s == 0:
                     spread_bias()
+
+            half = NODES // 2
+            second_matmul(last - 2)
+            scale_adj(last, 0, half)
+            regroup_whole(last - 1)
+            scale_adj(last, half, half)
+            bias_relu(last - 2)
+            round_z(last)
+            for i0 in (0, half):
+                ag_half = work.tile([P, half, PACK], BF16, align_bytes=64)
+                a_grouped[last, i0] = ag_half
+            regroup_a(last, 0, 0, TAIL_COLS, on_scalar)
+            regroup_a(last, 0, TAIL_COLS, half, on_gpsimd)
+            transpose_back_and_store(last - 3)
+            quantise_z(last)
+            regroup_a(last, half, 0, TAIL_COLS, on_vector)
+            regroup_a(last, half, TAIL_COLS, half, on_scalar)
+            quantise_a(last - 1)
+            transpose_back_and_store(last - 2)
+            second_matmul(last - 1)
+            bias_relu(last - 1)
+            for i0 in (0, half):
+                quantise_a(last, i0, half)
+                out_t_half = psum.tile([P, half], F32, tag="d_row", bufs=2)
+                multiply_a_z(last, i0, out_t_half)
+            for i0 in (0, half):
+                rt_half = work.tile([P, 2, P], F32)
+                nc.vector.tensor_scalar(
+                    out=rt_half[:], in0=out_t_sums[last, i0][:].rearrange("h (m f) -> h f m", f=2),
+                    scalar1=bias_col[:, 0:1], scalar2=0.0, op0=ALU.add, op1=ALU.max,
+                )
+                relu_t[last, i0] = rt_half
+            out_a = psum.tile([P, 2, HIDDEN], F32, tag="xt0")
+            transpose_back(last, 0, out_a, on_vector)
+            transpose_back_and_store(last - 1)
+            out_b = psum.tile([P, 2, HIDDEN], F32, tag="xt1")
+            transpose_back(last, half, out_b, on_vector)

@@ -21,7 +21,7 @@ NODE_TILES = NODES // P
 
 FLOPS = 2 * GRAPHS * NODES * (FEATS + NODES) * HIDDEN
 
-S_COLS = 192
+S_COLS = 160
 
 TAIL_COLS = 160
 
@@ -211,10 +211,15 @@ def tile_perception_pa_t_kernel(tc, batch_graph, adj, W1, b1, out):
             a_slots[b, i0] = a_rows
 
         def regroup_a(b, i0, lo, hi, copy_on):
-            copy_on(
-                a_grouped[b, i0][:, lo:hi, :].rearrange("p (c i) t -> p c t i", i=4),
-                a_slots[b, i0][:, :, lo:hi].rearrange("p t (c i) -> p c t i", i=4),
-            )
+            dst = a_grouped[b, i0][:, lo:hi, :]
+            src = a_slots[b, i0][:, :, lo:hi]
+            if copy_on is on_gpsimd:
+                copy_on(dst, src.rearrange("p t i -> p i t"))
+            else:
+                copy_on(
+                    dst.rearrange("p (c i) t -> p c t i", i=4),
+                    src.rearrange("p t (c i) -> p c t i", i=4),
+                )
 
         def on_scalar(dst, src):
             nc.scalar.copy(out=dst, in_=src)

@@ -21,11 +21,14 @@ NODE_TILES = NODES // P
 
 FLOPS = 2 * GRAPHS * NODES * (FEATS + NODES) * HIDDEN
 
-S_COLS = 160
+S_COLS = 144
 
-TAIL_COLS = 160
+TAIL_COLS = 192
+TAIL_COLS_2 = 160
 
 DEG_COLS = 24
+
+X_SHIFT = 1
 
 LOAD_AHEAD = 4
 
@@ -85,7 +88,7 @@ def tile_perception_pa_t_kernel(tc, batch_graph, adj, W1, b1, out):
         def spread_bias():
             bias_ps = psum.tile([P, DEG_COLS], F32, tag="out_ps")
             nc.tensor.matmul(bias_ps[:], lhsT=bias_rows[:], rhs=ones[:], start=True, stop=True)
-            nc.vector.tensor_copy(out=bias_col[:], in_=bias_ps[:, 0:1])
+            nc.scalar.copy(out=bias_col[:], in_=bias_ps[:, 0:1])
 
         w_grouped = const.tile([P, HIDDEN, PACK], BF16, align_bytes=64)
         nc.vector.tensor_copy(out=w_grouped[:], in_=w_rows[:].rearrange("q t h -> q h t"))
@@ -101,11 +104,11 @@ def tile_perception_pa_t_kernel(tc, batch_graph, adj, W1, b1, out):
         deg_sums, deg_root, deg_col, deg_row = {}, {}, {}, {}
         z_sums, z_grouped, z_quant = {}, {}, {}
         a_slots, a_grouped, a_quant = {}, {}, {}
-        out_t_sums, relu_t = {}, {}
+        out_t_sums, relu_t, out_sums = {}, {}, {}
 
         def transpose_x(b):
             x_words = x_sb[b][:].bitcast(F32)
-            grouped = work.tile([P, NODES, PACK], BF16, align_bytes=64)
+            grouped = work.tile([P, NODES, PACK], BF16, align_bytes=64, bufs=3)
             grouped_words = grouped[:].bitcast(F32).rearrange("w (q s) u -> w q s u", s=PACK)
             for half in range(2):
                 xt = psum.tile([P, 2, 2, P], F32, tag="xt%d" % half)
@@ -201,7 +204,7 @@ def tile_perception_pa_t_kernel(tc, batch_graph, adj, W1, b1, out):
             deg_row[b] = d_row
 
         def scale_adj(b, i0=0, n=NODES):
-            a_rows = work.tile([P, PACK, n], BF16)
+            a_rows = work.tile([P, PACK, n], BF16, bufs=3)
             for t in range(PACK):
                 nc.vector.scalar_tensor_tensor(
                     out=a_rows[:, t, :], in0=adj_sb[b][:, t, i0 : i0 + n],
@@ -233,14 +236,15 @@ def tile_perception_pa_t_kernel(tc, batch_graph, adj, W1, b1, out):
             )
 
         def regroup_whole(b):
-            ag = work.tile([P, NODES, PACK], BF16, align_bytes=64, bufs=1)
-            a_grouped[b, 0] = ag
+            if b > 0:
+                ag = work.tile([P, NODES, PACK], BF16, align_bytes=64, bufs=1)
+                a_grouped[b, 0] = ag
             regroup_a(b, 0, 0, S_COLS, on_scalar)
             regroup_a(b, 0, S_COLS, NODES, on_gpsimd)
 
         def quantise_a(b, i0=0, n=NODES):
-            a_codes = work.tile([P, n], U32, align_bytes=64)
-            a_scales = work.tile([P, n], U8, align_bytes=64)
+            a_codes = work.tile([P, n], U32, align_bytes=64, bufs=3)
+            a_scales = work.tile([P, n], U8, align_bytes=64, bufs=3)
             nc.vector.quantize_mx(
                 out=a_codes[:].bitcast(FP8X4),
                 scales=a_scales[:],
@@ -274,19 +278,23 @@ def tile_perception_pa_t_kernel(tc, batch_graph, adj, W1, b1, out):
             )
             relu_t[b, 0] = rt
 
-        def transpose_back(b, i0, out_ps, copy_on):
-            r = out_ps.shape[1]
-            for f in range(r):
+        def transpose_back(b, i0, out_ps):
+            for f in range(out_ps.shape[1]):
                 nc.tensor.transpose(out_ps[:, f, :], relu_t[b, i0][:, f, :], ident[:])
-            result = work.tile([P, r, HIDDEN], F32, bufs=3)
-            copy_on(result[:], out_ps[:])
+            out_sums[b, i0] = out_ps
+
+        def store(b, i0, copy_on):
+            r = out_sums[b, i0].shape[1]
+            result = work.tile([P, r, HIDDEN], F32, bufs=6)
+            copy_on(result[:], out_sums[b, i0][:])
             nc.sync.dma_start(
                 out=out[b, i0 : i0 + r * P, :].rearrange("(m f) h -> m f h", f=r), in_=result[:]
             )
 
         def transpose_back_and_store(b):
             out_ps = psum.tile([P, NODE_TILES, HIDDEN], F32)
-            transpose_back(b, 0, out_ps, on_scalar)
+            transpose_back(b, 0, out_ps)
+            store(b, 0, on_scalar)
 
         def run(piece, b):
             if 0 <= b < GRAPHS:
@@ -300,63 +308,86 @@ def tile_perception_pa_t_kernel(tc, batch_graph, adj, W1, b1, out):
             transpose_x(0)
             sum_degrees(1)
             root_degrees(1)
+            spread_degrees(1)
             transpose_x(1)
 
             last = GRAPHS - 1
-            for s in range(last):
+            run(load_adj, 1 + LOAD_AHEAD)
+            run(load_x, LOAD_AHEAD)
+            scale_adj(0)
+            quantise_x(0)
+            mask_degrees(1)
+            ag = work.tile([P, NODES, PACK], BF16, align_bytes=64, bufs=1)
+            a_grouped[0, 0] = ag
+            nc.vector.memset(ag[:, NODES - 4 : NODES, :], 0.0)
+            first_matmul(0)
+            regroup_whole(0)
+            sum_degrees(2)
+            root_degrees(2)
+            round_z(0)
+            transpose_x(2)
+
+            for s in range(1, last):
                 run(load_adj, s + 1 + LOAD_AHEAD)
                 run(load_x, s + LOAD_AHEAD)
                 run(second_matmul, s - 2)
                 run(spread_degrees, s + 1)
+                if s == X_SHIFT + 1:
+                    round_z(X_SHIFT)
+                    first_matmul(X_SHIFT + 1)
                 run(scale_adj, s)
-                run(regroup_whole, s - 1)
+                if s > 1:
+                    regroup_whole(s - 1)
                 run(bias_relu, s - 2)
-                if s == 0:
-                    quantise_x(0)
-                if s == 1:
-                    round_z(0)
-                    first_matmul(1)
-                if s > 0:
+                if s > X_SHIFT:
                     round_z(s)
+                if s == 1:
+                    spread_bias()
+                if s <= X_SHIFT:
+                    quantise_x(s)
                 run(mask_degrees, s + 1)
                 run(transpose_x, s + 2)
-                run(quantise_x, s + 1)
+                if s >= X_SHIFT:
+                    run(quantise_x, s + 1)
                 run(transpose_back_and_store, s - 3)
                 run(sum_degrees, s + 2)
                 run(root_degrees, s + 2)
-                if s == 1:
-                    quantise_z(0)
-                if s > 0:
+                if s <= X_SHIFT + 1:
+                    quantise_z(s - 1)
+                if s > X_SHIFT:
                     quantise_z(s)
                 run(quantise_a, s - 1)
-                first_matmul(0 if s == 0 else s + 1)
-                if s == 0:
-                    spread_bias()
+                first_matmul(s if s <= X_SHIFT else s + 1)
 
             half = NODES // 2
             second_matmul(last - 2)
             scale_adj(last, 0, half)
             regroup_whole(last - 1)
             scale_adj(last, half, half)
-            bias_relu(last - 2)
-            round_z(last)
             for i0 in (0, half):
                 ag_half = work.tile([P, half, PACK], BF16, align_bytes=64)
                 a_grouped[last, i0] = ag_half
-            regroup_a(last, 0, 0, TAIL_COLS, on_scalar)
-            regroup_a(last, 0, TAIL_COLS, half, on_gpsimd)
-            transpose_back_and_store(last - 3)
-            quantise_z(last)
-            regroup_a(last, half, 0, TAIL_COLS, on_vector)
-            regroup_a(last, half, TAIL_COLS, half, on_scalar)
+            round_z(last)
+            bias_relu(last - 2)
             quantise_a(last - 1)
-            transpose_back_and_store(last - 2)
+            regroup_a(last, 0, 0, TAIL_COLS, on_scalar)
+            if TAIL_COLS < half:
+                regroup_a(last, 0, TAIL_COLS, half, on_vector)
+            regroup_a(last, half, 0, TAIL_COLS_2, on_vector)
+            regroup_a(last, half, TAIL_COLS_2, half, on_scalar)
+            transpose_back_and_store(last - 3)
+            out_late = psum.tile([P, NODE_TILES, HIDDEN], F32, tag="xt0")
+            transpose_back(last - 2, 0, out_late)
             second_matmul(last - 1)
             bias_relu(last - 1)
+            store(last - 2, 0, on_scalar)
+            quantise_z(last)
             for i0 in (0, half):
                 quantise_a(last, i0, half)
                 out_t_half = psum.tile([P, half], F32, tag="d_row", bufs=2)
                 multiply_a_z(last, i0, out_t_half)
+            out_late = psum.tile([P, NODE_TILES, HIDDEN], F32, tag="z_ps")
+            transpose_back(last - 1, 0, out_late)
             for i0 in (0, half):
                 rt_half = work.tile([P, 2, P], F32)
                 nc.vector.tensor_scalar(
@@ -364,8 +395,10 @@ def tile_perception_pa_t_kernel(tc, batch_graph, adj, W1, b1, out):
                     scalar1=bias_col[:, 0:1], scalar2=0.0, op0=ALU.add, op1=ALU.max,
                 )
                 relu_t[last, i0] = rt_half
-            out_a = psum.tile([P, 2, HIDDEN], F32, tag="xt0")
-            transpose_back(last, 0, out_a, on_vector)
-            transpose_back_and_store(last - 1)
-            out_b = psum.tile([P, 2, HIDDEN], F32, tag="xt1")
-            transpose_back(last, half, out_b, on_vector)
+            out_half = psum.tile([P, 2, HIDDEN], F32, tag="xt1")
+            transpose_back(last, 0, out_half)
+            store(last, 0, on_vector)
+            store(last - 1, 0, on_scalar)
+            out_half = psum.tile([P, 2, HIDDEN], F32, tag="deg_ps")
+            transpose_back(last, half, out_half)
+            store(last, half, on_vector)

@@ -21,14 +21,14 @@ NODE_TILES = NODES // P
 
 FLOPS = 2 * GRAPHS * NODES * (FEATS + NODES) * HIDDEN
 
-S_COLS = 144
+S_COLS = 160
 
 TAIL_COLS = 192
 TAIL_COLS_2 = 160
 
 DEG_COLS = 24
 
-X_SHIFT = 1
+X_SHIFT = 2
 
 LOAD_AHEAD = 4
 
@@ -101,7 +101,7 @@ def tile_perception_pa_t_kernel(tc, batch_graph, adj, W1, b1, out):
         )
 
         x_grouped, x_quant = {}, {}
-        deg_sums, deg_root, deg_col, deg_row = {}, {}, {}, {}
+        deg_sums, deg_root, deg_roots, deg_col, deg_row = {}, {}, {}, {}, {}
         z_sums, z_grouped, z_quant = {}, {}, {}
         a_slots, a_grouped, a_quant = {}, {}, {}
         out_t_sums, relu_t, out_sums = {}, {}, {}
@@ -165,33 +165,38 @@ def tile_perception_pa_t_kernel(tc, batch_graph, adj, W1, b1, out):
             )
             z_quant[b] = (z_codes, z_scales)
 
-        def sum_degrees(b):
-            deg_ps = psum.tile([P, NODE_TILES, DEG_COLS], F32)
-            for f in range(NODE_TILES):
-                for t in range(PACK):
-                    nc.tensor.matmul(
-                        deg_ps[:, f, :],
-                        lhsT=adj_sb[b][:, t, P * f : P * f + P],
-                        rhs=ones[:],
-                        start=(t == 0),
-                        stop=(t == PACK - 1),
-                    )
-            deg_sums[b] = deg_ps[:, :, 0]
+        def sum_degrees(*graphs):
+            deg_ps = psum.tile([P, len(graphs) * NODE_TILES, DEG_COLS], F32)
+            for h, b in enumerate(graphs):
+                for f in range(NODE_TILES):
+                    for t in range(PACK):
+                        nc.tensor.matmul(
+                            deg_ps[:, h * NODE_TILES + f, :],
+                            lhsT=adj_sb[b][:, t, P * f : P * f + P],
+                            rhs=ones[:],
+                            start=(t == 0),
+                            stop=(t == PACK - 1),
+                        )
+            deg_sums[graphs] = deg_ps[:, :, 0]
 
-        def root_degrees(b):
-            inv_root = small.tile([P, NODE_TILES], F32)
+        def root_degrees(*graphs):
+            inv_root = small.tile([P, len(graphs) * NODE_TILES], F32)
             nc.scalar.activation(
-                out=inv_root[:], in_=deg_sums[b], func=ACT.Abs_reciprocal_sqrt, scale=1.0, bias=1e-30
+                out=inv_root[:], in_=deg_sums[graphs], func=ACT.Abs_reciprocal_sqrt,
+                scale=1.0, bias=1e-30,
             )
-            deg_root[b] = inv_root
+            deg_roots[graphs] = inv_root
+            for h, b in enumerate(graphs):
+                deg_root[b] = inv_root[:, h * NODE_TILES : (h + 1) * NODE_TILES]
 
-        def mask_degrees(b):
-            d_col = small.tile([P, NODE_TILES], F32)
+        def mask_degrees(*graphs):
+            d_col = small.tile([P, len(graphs) * NODE_TILES], F32)
             nc.vector.scalar_tensor_tensor(
-                out=d_col[:], in0=deg_sums[b], scalar=0.0, in1=deg_root[b][:],
+                out=d_col[:], in0=deg_sums[graphs], scalar=0.0, in1=deg_roots[graphs][:],
                 op0=ALU.is_gt, op1=ALU.mult,
             )
-            deg_col[b] = d_col
+            for h, b in enumerate(graphs):
+                deg_col[b] = d_col[:, h * NODE_TILES : (h + 1) * NODE_TILES]
 
         def spread_degrees(b):
             d_row = psum.tile([P, NODES], F32, bufs=2)
@@ -341,17 +346,26 @@ def tile_perception_pa_t_kernel(tc, batch_graph, adj, W1, b1, out):
                 run(bias_relu, s - 2)
                 if s > X_SHIFT:
                     round_z(s)
+                elif s > 1:
+                    round_z(s - 1)
                 if s == 1:
                     spread_bias()
                 if s <= X_SHIFT:
                     quantise_x(s)
-                run(mask_degrees, s + 1)
+                if s <= 3 or s == last - 1:
+                    mask_degrees(s + 1)
+                elif s % 2 == 0:
+                    mask_degrees(s + 1, s + 2)
                 run(transpose_x, s + 2)
                 if s >= X_SHIFT:
                     run(quantise_x, s + 1)
                 run(transpose_back_and_store, s - 3)
-                run(sum_degrees, s + 2)
-                run(root_degrees, s + 2)
+                if s <= 2 or s == last - 2:
+                    sum_degrees(s + 2)
+                    root_degrees(s + 2)
+                elif s % 2 == 1 and s + 3 <= last:
+                    sum_degrees(s + 2, s + 3)
+                    root_degrees(s + 2, s + 3)
                 if s <= X_SHIFT + 1:
                     quantise_z(s - 1)
                 if s > X_SHIFT:

@@ -30,7 +30,7 @@ DEG_COLS = 24
 
 X_SHIFT = 2
 
-LOAD_AHEAD = 4
+LOAD_AHEAD = 6
 
 
 def tile_perception_pa_t_kernel(tc, batch_graph, adj, W1, b1, out):
@@ -100,6 +100,7 @@ def tile_perception_pa_t_kernel(tc, batch_graph, adj, W1, b1, out):
             in_=w_grouped[:].rearrange("q h t -> q (h t)"),
         )
 
+        z_late = (4, 6, 8, 10, 12, 14)
         x_grouped, x_quant = {}, {}
         deg_sums, deg_root, deg_roots, deg_col, deg_row = {}, {}, {}, {}, {}
         z_sums, z_grouped, z_quant = {}, {}, {}
@@ -151,19 +152,28 @@ def tile_perception_pa_t_kernel(tc, batch_graph, adj, W1, b1, out):
             z_sums[b] = z_ps
 
         def round_z(b):
-            zg = work.tile([P, HIDDEN, PACK], BF16, align_bytes=64)
-            nc.scalar.copy(out=zg[:], in_=z_sums[b][:].rearrange("p t h -> p h t"))
+            if b in z_late:
+                zg = z_grouped[b - 1]
+            else:
+                zg = work.tile([P, 2 if b + 1 in z_late else 1, HIDDEN, PACK], BF16, align_bytes=64)
             z_grouped[b] = zg
+            nc.scalar.copy(
+                out=zg[:, 1 if b in z_late else 0, :, :],
+                in_=z_sums[b][:].rearrange("p t h -> p h t"),
+            )
 
-        def quantise_z(b):
-            z_codes = work.tile([P, HIDDEN], U32, align_bytes=64, bufs=3)
-            z_scales = work.tile([P, HIDDEN], U8, align_bytes=64, bufs=3)
+        def quantise_z(*graphs):
+            n = len(graphs) * HIDDEN
+            z_codes = work.tile([P, n], U32, align_bytes=64, bufs=3)
+            z_scales = work.tile([P, n], U8, align_bytes=64, bufs=3)
             nc.vector.quantize_mx(
                 out=z_codes[:].bitcast(FP8X4),
                 scales=z_scales[:],
-                in_=z_grouped[b][:].rearrange("p h t -> p (h t)"),
+                in_=z_grouped[graphs[0]][:].rearrange("p g h t -> p (g h t)"),
             )
-            z_quant[b] = (z_codes, z_scales)
+            for k, b in enumerate(graphs):
+                cols = slice(k * HIDDEN, k * HIDDEN + HIDDEN)
+                z_quant[b] = (z_codes[:, cols], z_scales[:, cols])
 
         def sum_degrees(*graphs):
             deg_ps = psum.tile([P, len(graphs) * NODE_TILES, DEG_COLS], F32)
@@ -262,8 +272,8 @@ def tile_perception_pa_t_kernel(tc, batch_graph, adj, W1, b1, out):
             a_codes, a_scales = a_quant[b, i0]
             nc.tensor.matmul_mx(
                 out=out_t_ps[:],
-                lhsT=z_codes[:].bitcast(FP8X4),
-                lhsT_scale=z_scales[:],
+                lhsT=z_codes.bitcast(FP8X4),
+                lhsT_scale=z_scales,
                 rhs=a_codes[:].bitcast(FP8X4),
                 rhs_scale=a_scales[:],
                 start=True,
@@ -368,8 +378,8 @@ def tile_perception_pa_t_kernel(tc, batch_graph, adj, W1, b1, out):
                     root_degrees(s + 2, s + 3)
                 if s <= X_SHIFT + 1:
                     quantise_z(s - 1)
-                if s > X_SHIFT:
-                    quantise_z(s)
+                if s in z_late:
+                    quantise_z(s - 1, s)
                 run(quantise_a, s - 1)
                 first_matmul(s if s <= X_SHIFT else s + 1)
 

from contextlib import ExitStack

import concourse.mybir as mybir
from concourse.masks import make_identity

F32 = mybir.dt.float32
BF16 = mybir.dt.bfloat16
U32 = mybir.dt.uint32
U8 = mybir.dt.uint8
FP8X4 = mybir.dt.float8_e4m3fn_x4
ALU = mybir.AluOpType
ACT = mybir.ActivationFunctionType

P = 128
PACK = 4
GRAPHS = 16
NODES = 512
FEATS = 512
HIDDEN = 128
NODE_TILES = NODES // P

FLOPS = 2 * GRAPHS * NODES * (FEATS + NODES) * HIDDEN

S_COLS = 160

TAIL_COLS = 192
TAIL_COLS_2 = 160

DEG_COLS = 24

X_SHIFT = 2

LOAD_AHEAD = 6


def tile_perception_pa_t_kernel(tc, batch_graph, adj, W1, b1, out):
    nc = tc.nc
    with ExitStack() as ctx:
        const = ctx.enter_context(tc.tile_pool(name="const", bufs=1))
        inputs = ctx.enter_context(tc.tile_pool(name="inputs", bufs=GRAPHS))
        work = ctx.enter_context(tc.tile_pool(name="work", bufs=2))
        small = ctx.enter_context(tc.tile_pool(name="small", bufs=4))
        psum = ctx.enter_context(tc.psum_pool(name="psum", bufs=1))

        adj_sb = {}
        x_sb = {}

        def load_adj(b):
            adj_rows = inputs.tile([P, PACK, NODES], BF16)
            nc.sync.dma_start(out=adj_rows[:], in_=adj[b].rearrange("(t p) i -> p t i", p=P))
            adj_sb[b] = adj_rows

        def load_x(b):
            x_rows = inputs.tile([P, PACK, FEATS], BF16)
            nc.sync.dma_start(
                out=x_rows[:], in_=batch_graph[b].rearrange("(q s) d -> q s d", s=PACK)
            )
            x_sb[b] = x_rows

        load_adj(0)
        w_rows = const.tile([P, PACK, HIDDEN], BF16)
        for u in range(2):
            nc.sync.dma_start(
                out=w_rows[:, 2 * u : 2 * u + 2, :],
                in_=W1[256 * u : 256 * u + 256, :].rearrange("(q e) h -> q e h", e=2),
            )
        bias_rows = const.tile([P, HIDDEN], BF16)
        nc.vector.memset(bias_rows[:], 0.0)
        nc.scalar.dma_start(out=bias_rows[0:1, :], in_=b1.rearrange("(o h) -> o h", o=1))
        for b in range(LOAD_AHEAD):
            load_x(b)
            load_adj(b + 1)

        ident = const.tile([P, P], F32)
        make_identity(nc, ident[:])
        ones = const.tile([P, DEG_COLS], BF16)
        nc.vector.memset(ones[:], 1.0)

        one_col = const.tile([P, 1], F32)
        nc.vector.memset(one_col[:], 1.0)
        root_of_one = const.tile([P, 1], F32)
        nc.scalar.activation(
            out=root_of_one[:], in_=one_col[:], func=ACT.Abs_reciprocal_sqrt, scale=1.0, bias=0.0
        )

        bias_col = const.tile([P, 1], F32)

        def spread_bias():
            bias_ps = psum.tile([P, DEG_COLS], F32, tag="out_ps")
            nc.tensor.matmul(bias_ps[:], lhsT=bias_rows[:], rhs=ones[:], start=True, stop=True)
            nc.scalar.copy(out=bias_col[:], in_=bias_ps[:, 0:1])

        w_grouped = const.tile([P, HIDDEN, PACK], BF16, align_bytes=64)
        nc.vector.tensor_copy(out=w_grouped[:], in_=w_rows[:].rearrange("q t h -> q h t"))
        w_codes = const.tile([P, HIDDEN], U32, align_bytes=64)
        w_scales = const.tile([P, HIDDEN], U8, align_bytes=64)
        nc.vector.quantize_mx(
            out=w_codes[:].bitcast(FP8X4),
            scales=w_scales[:],
            in_=w_grouped[:].rearrange("q h t -> q (h t)"),
        )

        z_late = (4, 6, 8, 10, 12, 14)
        x_grouped, x_quant = {}, {}
        deg_sums, deg_root, deg_roots, deg_col, deg_row = {}, {}, {}, {}, {}
        z_sums, z_grouped, z_quant = {}, {}, {}
        a_slots, a_grouped, a_quant = {}, {}, {}
        out_t_sums, relu_t, out_sums = {}, {}, {}

        def transpose_x(b):
            x_words = x_sb[b][:].bitcast(F32)
            grouped = work.tile([P, NODES, PACK], BF16, align_bytes=64, bufs=3)
            grouped_words = grouped[:].bitcast(F32).rearrange("w (q s) u -> w q s u", s=PACK)
            for half in range(2):
                xt = psum.tile([P, 2, 2, P], F32, tag="xt%d" % half)
                for s2 in range(2):
                    for u in range(2):
                        nc.tensor.transpose(
                            xt[:, s2, u, :],
                            x_words[:, 2 * half + s2, P * u : P * u + P],
                            ident[:],
                        )
                nc.scalar.copy(
                    out=grouped_words[:, :, 2 * half : 2 * half + 2, :],
                    in_=xt[:].rearrange("w s u q -> w q s u"),
                )
            x_grouped[b] = grouped

        def quantise_x(b):
            x_codes = work.tile([P, NODES], U32, align_bytes=64)
            x_scales = work.tile([P, NODES], U8, align_bytes=64)
            nc.vector.quantize_mx(
                out=x_codes[:].bitcast(FP8X4),
                scales=x_scales[:],
                in_=x_grouped[b][:].rearrange("w n t -> w (n t)"),
            )
            x_quant[b] = (x_codes, x_scales)

        def first_matmul(b):
            x_codes, x_scales = x_quant[b]
            z_ps = psum.tile([P, PACK, HIDDEN], F32)
            for t in range(PACK):
                nc.tensor.matmul_mx(
                    out=z_ps[:, t, :],
                    lhsT=x_codes[:, P * t : P * t + P].bitcast(FP8X4),
                    lhsT_scale=x_scales[:, P * t : P * t + P],
                    rhs=w_codes[:].bitcast(FP8X4),
                    rhs_scale=w_scales[:],
                    start=True,
                    stop=True,
                )
            z_sums[b] = z_ps

        def round_z(b):
            if b in z_late:
                zg = z_grouped[b - 1]
            else:
                zg = work.tile([P, 2 if b + 1 in z_late else 1, HIDDEN, PACK], BF16, align_bytes=64)
            z_grouped[b] = zg
            nc.scalar.copy(
                out=zg[:, 1 if b in z_late else 0, :, :],
                in_=z_sums[b][:].rearrange("p t h -> p h t"),
            )

        def quantise_z(*graphs):
            n = len(graphs) * HIDDEN
            z_codes = work.tile([P, n], U32, align_bytes=64, bufs=3)
            z_scales = work.tile([P, n], U8, align_bytes=64, bufs=3)
            nc.vector.quantize_mx(
                out=z_codes[:].bitcast(FP8X4),
                scales=z_scales[:],
                in_=z_grouped[graphs[0]][:].rearrange("p g h t -> p (g h t)"),
            )
            for k, b in enumerate(graphs):
                cols = slice(k * HIDDEN, k * HIDDEN + HIDDEN)
                z_quant[b] = (z_codes[:, cols], z_scales[:, cols])

        def sum_degrees(*graphs):
            deg_ps = psum.tile([P, len(graphs) * NODE_TILES, DEG_COLS], F32)
            for h, b in enumerate(graphs):
                for f in range(NODE_TILES):
                    for t in range(PACK):
                        nc.tensor.matmul(
                            deg_ps[:, h * NODE_TILES + f, :],
                            lhsT=adj_sb[b][:, t, P * f : P * f + P],
                            rhs=ones[:],
                            start=(t == 0),
                            stop=(t == PACK - 1),
                        )
            deg_sums[graphs] = deg_ps[:, :, 0]

        def root_degrees(*graphs):
            inv_root = small.tile([P, len(graphs) * NODE_TILES], F32)
            nc.scalar.activation(
                out=inv_root[:], in_=deg_sums[graphs], func=ACT.Abs_reciprocal_sqrt,
                scale=1.0, bias=1e-30,
            )
            deg_roots[graphs] = inv_root
            for h, b in enumerate(graphs):
                deg_root[b] = inv_root[:, h * NODE_TILES : (h + 1) * NODE_TILES]

        def mask_degrees(*graphs):
            d_col = small.tile([P, len(graphs) * NODE_TILES], F32)
            nc.vector.scalar_tensor_tensor(
                out=d_col[:], in0=deg_sums[graphs], scalar=0.0, in1=deg_roots[graphs][:],
                op0=ALU.is_gt, op1=ALU.mult,
            )
            for h, b in enumerate(graphs):
                deg_col[b] = d_col[:, h * NODE_TILES : (h + 1) * NODE_TILES]

        def spread_degrees(b):
            d_row = psum.tile([P, NODES], F32, bufs=2)
            for f in range(NODE_TILES):
                nc.tensor.transpose(
                    d_row[:, P * f : P * f + P],
                    deg_root[b][:, f : f + 1].to_broadcast([P, P]),
                    ident[:],
                )
            deg_row[b] = d_row

        def scale_adj(b, i0=0, n=NODES):
            a_rows = work.tile([P, PACK, n], BF16, bufs=3)
            for t in range(PACK):
                nc.vector.scalar_tensor_tensor(
                    out=a_rows[:, t, :], in0=adj_sb[b][:, t, i0 : i0 + n],
                    scalar=deg_col[b][:, t : t + 1], in1=deg_row[b][:, i0 : i0 + n],
                    op0=ALU.mult, op1=ALU.mult,
                )
            a_slots[b, i0] = a_rows

        def regroup_a(b, i0, lo, hi, copy_on):
            dst = a_grouped[b, i0][:, lo:hi, :]
            src = a_slots[b, i0][:, :, lo:hi]
            if copy_on is on_gpsimd:
                copy_on(dst, src.rearrange("p t i -> p i t"))
            else:
                copy_on(
                    dst.rearrange("p (c i) t -> p c t i", i=4),
                    src.rearrange("p t (c i) -> p c t i", i=4),
                )

        def on_scalar(dst, src):
            nc.scalar.copy(out=dst, in_=src)

        def on_vector(dst, src):
            nc.vector.tensor_copy(out=dst, in_=src)

        def on_gpsimd(dst, src):
            nc.gpsimd.tensor_scalar(
                out=dst, in0=src, scalar1=1.0, scalar2=0.0, op0=ALU.mult, op1=ALU.add
            )

        def regroup_whole(b):
            if b > 0:
                ag = work.tile([P, NODES, PACK], BF16, align_bytes=64, bufs=1)
                a_grouped[b, 0] = ag
            regroup_a(b, 0, 0, S_COLS, on_scalar)
            regroup_a(b, 0, S_COLS, NODES, on_gpsimd)

        def quantise_a(b, i0=0, n=NODES):
            a_codes = work.tile([P, n], U32, align_bytes=64, bufs=3)
            a_scales = work.tile([P, n], U8, align_bytes=64, bufs=3)
            nc.vector.quantize_mx(
                out=a_codes[:].bitcast(FP8X4),
                scales=a_scales[:],
                in_=a_grouped[b, i0][:].rearrange("p i t -> p (i t)"),
            )
            a_quant[b, i0] = (a_codes, a_scales)

        def multiply_a_z(b, i0, out_t_ps):
            z_codes, z_scales = z_quant[b]
            a_codes, a_scales = a_quant[b, i0]
            nc.tensor.matmul_mx(
                out=out_t_ps[:],
                lhsT=z_codes.bitcast(FP8X4),
                lhsT_scale=z_scales,
                rhs=a_codes[:].bitcast(FP8X4),
                rhs_scale=a_scales[:],
                start=True,
                stop=True,
            )
            out_t_sums[b, i0] = out_t_ps

        def second_matmul(b):
            out_t_ps = psum.tile([P, NODES], F32)
            multiply_a_z(b, 0, out_t_ps)

        def bias_relu(b):
            rt = work.tile([P, NODE_TILES, P], F32)
            nc.scalar.activation(
                out=rt[:], in_=out_t_sums[b, 0][:].rearrange("h (m f) -> h f m", f=NODE_TILES),
                func=ACT.Relu, bias=bias_col[:, 0:1], scale=1.0,
            )
            relu_t[b, 0] = rt

        def transpose_back(b, i0, out_ps):
            for f in range(out_ps.shape[1]):
                nc.tensor.transpose(out_ps[:, f, :], relu_t[b, i0][:, f, :], ident[:])
            out_sums[b, i0] = out_ps

        def store(b, i0, copy_on):
            r = out_sums[b, i0].shape[1]
            result = work.tile([P, r, HIDDEN], F32, bufs=6)
            copy_on(result[:], out_sums[b, i0][:])
            nc.sync.dma_start(
                out=out[b, i0 : i0 + r * P, :].rearrange("(m f) h -> m f h", f=r), in_=result[:]
            )

        def transpose_back_and_store(b):
            out_ps = psum.tile([P, NODE_TILES, HIDDEN], F32)
            transpose_back(b, 0, out_ps)
            store(b, 0, on_scalar)

        def run(piece, b):
            if 0 <= b < GRAPHS:
                piece(b)

        with tc.manual_schedule():
            sum_degrees(0)
            root_degrees(0)
            spread_degrees(0)
            mask_degrees(0)
            transpose_x(0)
            sum_degrees(1)
            root_degrees(1)
            spread_degrees(1)
            transpose_x(1)

            last = GRAPHS - 1
            run(load_adj, 1 + LOAD_AHEAD)
            run(load_x, LOAD_AHEAD)
            scale_adj(0)
            quantise_x(0)
            mask_degrees(1)
            ag = work.tile([P, NODES, PACK], BF16, align_bytes=64, bufs=1)
            a_grouped[0, 0] = ag
            nc.vector.memset(ag[:, NODES - 4 : NODES, :], 0.0)
            first_matmul(0)
            regroup_whole(0)
            sum_degrees(2)
            root_degrees(2)
            round_z(0)
            transpose_x(2)

            for s in range(1, last):
                run(load_adj, s + 1 + LOAD_AHEAD)
                run(load_x, s + LOAD_AHEAD)
                run(second_matmul, s - 2)
                run(spread_degrees, s + 1)
                if s == X_SHIFT + 1:
                    round_z(X_SHIFT)
                    first_matmul(X_SHIFT + 1)
                run(scale_adj, s)
                if s > 1:
                    regroup_whole(s - 1)
                run(bias_relu, s - 2)
                if s > X_SHIFT:
                    round_z(s)
                elif s > 1:
                    round_z(s - 1)
                if s == 1:
                    spread_bias()
                if s <= X_SHIFT:
                    quantise_x(s)
                if s <= 3 or s == last - 1:
                    mask_degrees(s + 1)
                elif s % 2 == 0:
                    mask_degrees(s + 1, s + 2)
                run(transpose_x, s + 2)
                if s >= X_SHIFT:
                    run(quantise_x, s + 1)
                run(transpose_back_and_store, s - 3)
                if s <= 2 or s == last - 2:
                    sum_degrees(s + 2)
                    root_degrees(s + 2)
                elif s % 2 == 1 and s + 3 <= last:
                    sum_degrees(s + 2, s + 3)
                    root_degrees(s + 2, s + 3)
                if s <= X_SHIFT + 1:
                    quantise_z(s - 1)
                if s in z_late:
                    quantise_z(s - 1, s)
                run(quantise_a, s - 1)
                first_matmul(s if s <= X_SHIFT else s + 1)

            half = NODES // 2
            second_matmul(last - 2)
            scale_adj(last, 0, half)
            regroup_whole(last - 1)
            scale_adj(last, half, half)
            for i0 in (0, half):
                ag_half = work.tile([P, half, PACK], BF16, align_bytes=64)
                a_grouped[last, i0] = ag_half
            round_z(last)
            bias_relu(last - 2)
            quantise_a(last - 1)
            regroup_a(last, 0, 0, TAIL_COLS, on_scalar)
            if TAIL_COLS < half:
                regroup_a(last, 0, TAIL_COLS, half, on_vector)
            regroup_a(last, half, 0, TAIL_COLS_2, on_vector)
            regroup_a(last, half, TAIL_COLS_2, half, on_scalar)
            transpose_back_and_store(last - 3)
            out_late = psum.tile([P, NODE_TILES, HIDDEN], F32, tag="xt0")
            transpose_back(last - 2, 0, out_late)
            second_matmul(last - 1)
            bias_relu(last - 1)
            store(last - 2, 0, on_scalar)
            quantise_z(last)
            for i0 in (0, half):
                quantise_a(last, i0, half)
                out_t_half = psum.tile([P, half], F32, tag="d_row", bufs=2)
                multiply_a_z(last, i0, out_t_half)
            out_late = psum.tile([P, NODE_TILES, HIDDEN], F32, tag="z_ps")
            transpose_back(last - 1, 0, out_late)
            for i0 in (0, half):
                rt_half = work.tile([P, 2, P], F32)
                nc.vector.tensor_scalar(
                    out=rt_half[:], in0=out_t_sums[last, i0][:].rearrange("h (m f) -> h f m", f=2),
                    scalar1=bias_col[:, 0:1], scalar2=0.0, op0=ALU.add, op1=ALU.max,
                )
                relu_t[last, i0] = rt_half
            out_half = psum.tile([P, 2, HIDDEN], F32, tag="xt1")
            transpose_back(last, 0, out_half)
            store(last, 0, on_vector)
            store(last - 1, 0, on_scalar)
            out_half = psum.tile([P, 2, HIDDEN], F32, tag="deg_ps")
            transpose_back(last, half, out_half)
            store(last, half, on_vector)
